import numpy as np
import ml_dtypes


def mxq(x, axis, fmt="e4m3"):
    dtype, down = {"e4m3": (ml_dtypes.float8_e4m3fn, 7), "e5m2": (ml_dtypes.float8_e5m2, 14)}[fmt]
    v = np.moveaxis(np.asarray(x, np.float32).astype(ml_dtypes.bfloat16).astype(np.float64), axis, -1)
    blocks = v.reshape(v.shape[:-1] + (-1, 32))
    amax = np.abs(blocks).max(-1, keepdims=True)
    byte = np.maximum(np.where(amax > 0, np.frexp(amax)[1] - 1 + 127, 0) - down, 1)
    scale = np.exp2(byte - 127.0)
    codes = (blocks / scale).astype(np.float32).astype(dtype).astype(np.float64)
    return np.moveaxis((codes * scale).reshape(v.shape), -1, axis)


WIDE = False


def mx_kscale(k):
    if not WIDE:
        return np.ones(k)
    levels = np.array([10, -10, 5, -5, 0])
    if k % 512:
        return np.exp2(np.random.permutation(np.resize(levels, k // 32))).repeat(32)
    a = np.empty((k // 512, 16))
    for p in range(k // 512):
        a[p, :8] = np.random.permutation(np.resize(levels, 8))
        for g in range(8):
            far = levels[np.abs(levels - a[p, g]) >= 10]
            a[p, g + 8] = far[np.random.randint(len(far))]
    return np.exp2(a.ravel()).repeat(32)


BF16 = ml_dtypes.bfloat16


def bf(x):
    return np.asarray(x, np.float32).astype(BF16)


def f64(x):
    return np.asarray(x).astype(np.float64)


B, Nb1, Nw1, Nb2x, Nb2y, Nw2x, Nw2y, R, C = 4096, 2, 16, 1, 1, 32, 16, 128, 2
J1 = Nb1 * Nb1
J3 = Nb2x * Nb2y
J2 = J3 * J1
K3 = J1 * R
L3 = C * Nw2x * Nw2y


def setup_inputs():
    t = mx_kscale(K3)
    tt = np.tile(t.reshape(J1, R), (J3, 1))
    return {"h_switch": bf(np.random.standard_normal((B, J2, R))),
            "k2": bf(np.random.standard_normal((J2, R, R)) / np.sqrt(R) * tt[:, None, :]),
            "b2": bf(np.random.standard_normal((1, J2, R)) * 0.3 * tt[None]),
            "k3": bf(np.random.standard_normal((J3, K3, L3)) / np.sqrt(K3) / t[None, :, None]),
            "b3": bf(np.random.standard_normal((1, J3, L3)) * 0.3)}


def reference(h_switch, k2, b2, k3, b3):
    g = (f64(h_switch).transpose(1, 0, 2) @ f64(k2)).transpose(1, 0, 2) + f64(b2)
    g = g.reshape(B, J3, K3)
    gq = mxq(g, 2, "e4m3").transpose(1, 0, 2)
    y = (gq @ mxq(f64(k3), 1, "e4m3")).transpose(1, 0, 2) + f64(b3)
    y = y.reshape(B, Nb2x, Nb2y, Nw2x, Nw2y, C).transpose(0, 1, 3, 2, 4, 5)
    return y.reshape(B, Nb2x * Nw2x, Nb2y * Nw2y, C)

@@ -1,0 +1,296 @@
+from contextlib import ExitStack
+
+import concourse.masks as masks
+import concourse.mybir as mybir
+
+BF16 = mybir.dt.bfloat16
+F32 = mybir.dt.float32
+U32 = mybir.dt.uint32
+U8 = mybir.dt.uint8
+I32 = mybir.dt.int32
+FP8X4 = mybir.dt.float8_e4m3fn_x4
+ADD = mybir.AluOpType.add
+
+P = 128
+GROUPS = 4
+K3 = GROUPS * P
+SAMPLES = 4096
+TILES = SAMPLES // P
+RT = 2
+RB = RT * P
+ROUNDS = TILES // RT
+L = 1024
+HALF = 512
+H_CHUNKS = [2, 2, 4, 8, 8, 8]
+
+FLOPS = 2 * SAMPLES * GROUPS * P * P + 2 * SAMPLES * GROUPS * P * L
+
+
+def tile_switchnet_fstar_pb_t_kernel(tc, h_switch, k2, b2, k3, b3, out):
+    nc = tc.nc
+    h_view = h_switch.rearrange("(p t) j r -> p t (j r)", t=TILES)
+    out_view = out.rearrange("(p t) x y c -> p t (x y c)", t=TILES)
+    k3_view = k3.rearrange("o (p j) n -> p (o j) n", j=4)
+
+    with ExitStack() as ctx:
+        ctx.enter_context(tc.manual_schedule())
+        const = ctx.enter_context(tc.tile_pool(name="const", bufs=1))
+        ht_pool = ctx.enter_context(tc.tile_pool(name="ht", bufs=3))
+        gs_pool = ctx.enter_context(tc.tile_pool(name="gs", bufs=3))
+        gb_pool = ctx.enter_context(tc.tile_pool(name="gb", bufs=3))
+        grp_pool = ctx.enter_context(tc.tile_pool(name="grp", bufs=3))
+        q_pool = ctx.enter_context(tc.tile_pool(name="q", bufs=3))
+        y_pool = ctx.enter_context(tc.tile_pool(name="ysb", bufs=5))
+        ps_t = ctx.enter_context(tc.psum_pool(name="pst", bufs=1))
+        ps_g = ctx.enter_context(tc.psum_pool(name="psg", bufs=2))
+        ps_w = ctx.enter_context(tc.psum_pool(name="psw", bufs=1))
+        ps_y = ctx.enter_context(tc.psum_pool(name="psy", bufs=4))
+
+        bz = const.tile([P, K3 + L], BF16, name="bz")
+        ones = const.tile([P, P], BF16, name="ones")
+        ident = const.tile([P, P], BF16, name="ident")
+        ident_f = const.tile([P, P], F32, name="identf")
+        warm = const.tile([P, 2], F32, name="warm")
+
+        h_of = []
+        h_tiles = []
+        t0 = 0
+        for c, n in enumerate(H_CHUNKS):
+            hc = const.tile([P, n, GROUPS * P], BF16, name="h%d" % c)
+            h_tiles.append((hc, t0, n))
+            for i in range(n):
+                h_of.append((hc, i))
+            t0 += n
+        k2_sb = const.tile([P, GROUPS, P], BF16, name="k2sb")
+        k3r = [const.tile([P, GROUPS, HALF], BF16, name="k3r%d" % i) for i in range(2)]
+        k3g = [const.tile([P, HALF, GROUPS], BF16, name="k3g%d" % i, align_bytes=64) for i in range(2)]
+        k3c = const.tile([P, L], U32, name="k3c", align_bytes=64)
+        k3s = const.tile([P, L], U8, name="k3s", align_bytes=64)
+        b2f = const.tile([P, K3], F32, name="b2f")
+        b3f = const.tile([P, L], F32, name="b3f")
+
+        def load_h(c):
+            hc, start, n = h_tiles[c]
+            nc.sync.dma_start(out=hc[:], in_=h_view[:, start:start + n, :])
+
+        def load_k3(i):
+            nc.sync.dma_start(out=k3r[i][:], in_=k3_view[:, :, i * HALF:(i + 1) * HALF])
+
+        nc.vector.memset(bz[:].bitcast(I32), 0)
+        nc.sync.dma_start(out=bz[0:1, 0:K3], in_=b2.rearrange("o j r -> o (j r)"))
+        nc.sync.dma_start(out=bz[0:1, K3:K3 + L], in_=b3.rearrange("o j l -> (o j) l"))
+        load_h(0)
+        nc.sync.dma_start(out=k2_sb[:], in_=k2.rearrange("j k m -> k j m"))
+        load_k3(0)
+        load_h(1)
+        load_k3(1)
+        for c in range(2, len(H_CHUNKS)):
+            load_h(c)
+
+        nc.vector.memset(ones[:], 1.0)
+        nc.vector.memset(warm[:], 0.0)
+        masks.make_identity(nc, ident[:])
+        masks.make_identity(nc, ident_f[:])
+        nc.scalar.copy(out=warm[:, 1:2], in_=warm[:, 0:1])
+
+        def spread(c0):
+            yb = ps_y.tile([P, HALF], F32, name="y", tag="y")
+            nc.tensor.matmul(yb[:], lhsT=ones[:], rhs=bz[:, c0:c0 + HALF], start=True, stop=True)
+            return yb
+
+        def by_words(ap):
+            return ap.rearrange("s (p u e) -> s u p e", u=2, e=2)
+
+        def in_words(ap):
+            return ap.rearrange("s (u p e) -> s u p e", u=2, e=2)
+
+        def regroup_k3(i):
+            nc.vector.tensor_copy(
+                out=k3g[i][:].rearrange("p (c i) t -> p c t i", i=4),
+                in_=k3r[i][:].rearrange("p t (c i) -> p c t i", i=4),
+            )
+
+        def quantise_k3(i):
+            nc.vector.quantize_mx(
+                out=k3c[:, i * HALF:(i + 1) * HALF].bitcast(FP8X4),
+                scales=k3s[:, i * HALF:(i + 1) * HALF],
+                in_=k3g[i][:].rearrange("p n t -> p (n t)"),
+            )
+
+        tps = {}
+        hts = {}
+        gps = {}
+        gss = {}
+        gbs = {}
+        wps = {}
+        grps = {}
+        qs = {}
+        yps = {}
+        ysbs = {}
+
+        def transposes(r):
+            tp = ps_t.tile([P, GROUPS, RT, P], BF16, name="tp", tag="tp")
+            for a in range(RT):
+                hc, off = h_of[RT * r + a]
+                for j in range(GROUPS):
+                    nc.tensor.transpose(tp[:, j, a, :], hc[:, off, j * P:(j + 1) * P], ident[:])
+            tps[r] = tp
+
+        def empty_t(r):
+            ht = ht_pool.tile([P, GROUPS, RT, P], BF16, name="ht", tag="ht")
+            nc.scalar.copy(out=ht[:], in_=tps[r][:])
+            hts[r] = ht
+
+        def stage1(r):
+            for a in range(RT):
+                g = ps_g.tile([P, K3], F32, name="g", tag="g")
+                for j in range(GROUPS):
+                    nc.tensor.matmul(g[:, j * P:(j + 1) * P], lhsT=hts[r][:, j, a, :], rhs=k2_sb[:, j, :],
+                                     start=True, stop=True)
+                gps[(r, a)] = g
+
+        def new_gb(r):
+            gbs[r] = gb_pool.tile([P, RT, K3], BF16, name="gb", tag="gb")
+
+        def add_b2_on_vector(r, a):
+            nc.vector.tensor_tensor(
+                out=in_words(gbs[r][:, a, :]), in0=by_words(gps[(r, a)][:]), in1=in_words(b2f[:]), op=ADD)
+
+        def empty_g(r):
+            gs = gs_pool.tile([P, RT, K3], F32, name="gs", tag="gs")
+            for a in range(RT):
+                nc.scalar.copy(out=in_words(gs[:, a, :]), in_=by_words(gps[(r, a)][:]))
+            gss[r] = gs
+
+        def add_b2(r):
+            new_gb(r)
+            nc.gpsimd.tensor_tensor(
+                out=gbs[r][:], in0=gss[r][:], in1=b2f[:].unsqueeze(1).to_broadcast([P, RT, K3]), op=ADD)
+
+        def words(r):
+            wp = ps_w.tile([P, RT, 2, P], F32, name="wp", tag="wp")
+            for a in range(RT):
+                w = gbs[r][:, a, :].bitcast(F32)
+                for u in range(2):
+                    nc.tensor.transpose(wp[:, a, u, :], w[:, u * P:(u + 1) * P], ident_f[:])
+            wps[r] = wp
+
+        def empty_w(r):
+            grp = grp_pool.tile([P, RT * P * 4], BF16, name="grp", tag="grp", align_bytes=64)
+            nc.scalar.copy(
+                out=grp[:].bitcast(F32).rearrange("p (a s u) -> p a s u", a=RT, u=2),
+                in_=wps[r][:].rearrange("p a u s -> p a s u"))
+            grps[r] = grp
+
+        def quantise(r):
+            codes = q_pool.tile([P, RB], U32, name="codes", tag="codes", align_bytes=64)
+            scl = q_pool.tile([P, RB], U8, name="scl", tag="scl", align_bytes=64)
+            nc.vector.quantize_mx(out=codes[:].bitcast(FP8X4), scales=scl[:], in_=grps[r][:])
+            qs[r] = (codes, scl)
+
+        def mx_pass(r, k):
+            a, i = k // 2, k % 2
+            codes, scl = qs[r]
+            y = ps_y.tile([P, HALF], F32, name="y", tag="y")
+            nc.tensor.matmul_mx(
+                out=y[:],
+                lhsT=codes[:, a * P:(a + 1) * P].bitcast(FP8X4),
+                lhsT_scale=scl[:, a * P:(a + 1) * P],
+                rhs=k3c[:, i * HALF:(i + 1) * HALF].bitcast(FP8X4),
+                rhs_scale=k3s[:, i * HALF:(i + 1) * HALF],
+                start=True,
+                stop=True,
+            )
+            yps[(r, k)] = y
+
+        def order(r):
+            return (0, 2, 1, 3) if r == 0 else (0, 1, 2, 3)
+
+        def empty_y(r, k):
+            a, i = k // 2, k % 2
+            if k == 0:
+                ysbs[r] = y_pool.tile([P, RT, L], F32, name="ysb", tag="ysb")
+            nc.vector.tensor_tensor(
+                out=ysbs[r][:, a, i * HALF:(i + 1) * HALF], in0=yps[(r, k)][:],
+                in1=b3f[:, i * HALF:(i + 1) * HALF], op=ADD)
+            t = RT * r + a
+            if r == ROUNDS - 1 and k == 1:
+                nc.sync.dma_start(out=out_view[:, t:t + 1, :], in_=ysbs[r][:, a:a + 1, :])
+            if r == ROUNDS - 1 and k >= 2:
+                nc.sync.dma_start(
+                    out=out_view[:, t:t + 1, i * HALF:(i + 1) * HALF],
+                    in_=ysbs[r][:, a:a + 1, i * HALF:(i + 1) * HALF])
+            if r < ROUNDS - 1 and k == 3:
+                nc.sync.dma_start(out=out_view[:, RT * r:RT * (r + 1), :], in_=ysbs[r][:])
+
+        yb2 = spread(0)
+        yb30 = spread(K3)
+        nc.vector.tensor_copy(out=in_words(b2f[:]), in_=by_words(yb2[:]))
+        nc.scalar.copy(out=b3f[:, 0:HALF], in_=yb30[:])
+        transposes(0)
+        empty_t(0)
+        yb31 = spread(K3 + HALF)
+        stage1(0)
+        nc.scalar.copy(out=b3f[:, HALF:L], in_=yb31[:])
+        transposes(1)
+        empty_t(1)
+        regroup_k3(0)
+        quantise_k3(0)
+        new_gb(0)
+        add_b2_on_vector(0, 0)
+        add_b2_on_vector(0, 1)
+        words(0)
+        empty_w(0)
+        stage1(1)
+        empty_g(1)
+        add_b2(1)
+        regroup_k3(1)
+        quantise(0)
+        quantise_k3(1)
+        transposes(2)
+        empty_t(2)
+        for k in order(0):
+            mx_pass(0, k)
+        stage1(2)
+        words(1)
+        empty_w(1)
+        empty_g(2)
+        add_b2(2)
+        transposes(3)
+        empty_t(3)
+        stage1(3)
+        empty_g(3)
+        transposes(4)
+        empty_t(4)
+        for s in range(ROUNDS):
+            late = s <= 1
+            k0, k1, k2_, k3_ = order(s)
+            if s + 2 < ROUNDS and not late:
+                words(s + 2)
+            if s + 5 < ROUNDS:
+                transposes(s + 5)
+            if s + 2 < ROUNDS and not late:
+                empty_w(s + 2)
+            if s + 5 < ROUNDS:
+                empty_t(s + 5)
+            empty_y(s, k0)
+            empty_y(s, k1)
+            if s + 1 < ROUNDS:
+                quantise(s + 1)
+            if s + 3 < ROUNDS:
+                add_b2(s + 3)
+            if s + 4 < ROUNDS:
+                stage1(s + 4)
+                empty_g(s + 4)
+            if s + 1 < ROUNDS:
+                mx_pass(s + 1, 0)
+                mx_pass(s + 1, 1)
+            empty_y(s, k2_)
+            if s + 1 < ROUNDS:
+                mx_pass(s + 1, 2)
+            empty_y(s, k3_)
+            if s + 1 < ROUNDS:
+                mx_pass(s + 1, 3)
+            if s + 2 < ROUNDS and late:
+                words(s + 2)
+                empty_w(s + 2)

@@ -10,6 +10,7 @@ U8 = mybir.dt.uint8
 I32 = mybir.dt.int32
 FP8X4 = mybir.dt.float8_e4m3fn_x4
 ADD = mybir.AluOpType.add
+MULT = mybir.AluOpType.mult
 
 P = 128
 GROUPS = 4
@@ -22,6 +23,14 @@ ROUNDS = TILES // RT
 L = 1024
 HALF = 512
 H_CHUNKS = [2, 2, 4, 8, 8, 8]
+PIECES = 1
+FINE = 3
+MODES = "VV" * 16
+
+
+def YM(r):
+    return "VVVV" if r < 1 else ("VSVS" if r < 15 else "SVVV")
+
 
 FLOPS = 2 * SAMPLES * GROUPS * P * P + 2 * SAMPLES * GROUPS * P * L
 
@@ -110,6 +119,12 @@ def tile_switchnet_fstar_pb_t_kernel(tc, h_switch, k2, b2, k3, b3, out):
                 in_=k3r[i][:].rearrange("p t (c i) -> p c t i", i=4),
             )
 
+        def regroup_k3_on_gpsimd(i, n0, n1):
+            nc.gpsimd.tensor_scalar(
+                out=k3g[i][:, n0:n1, :].rearrange("p (c i) t -> p c t i", i=4),
+                in0=k3r[i][:, :, n0:n1].rearrange("p t (c i) -> p c t i", i=4),
+                scalar1=1.0, scalar2=0.0, op0=MULT, op1=ADD)
+
         def quantise_k3(i):
             nc.vector.quantize_mx(
                 out=k3c[:, i * HALF:(i + 1) * HALF].bitcast(FP8X4),
@@ -128,8 +143,11 @@ def tile_switchnet_fstar_pb_t_kernel(tc, h_switch, k2, b2, k3, b3, out):
         yps = {}
         ysbs = {}
 
-        def transposes(r):
-            tp = ps_t.tile([P, GROUPS, RT, P], BF16, name="tp", tag="tp")
+        def transposes(r, spare=False):
+            if spare:
+                tp = ps_y.tile([P, GROUPS, RT, P], BF16, name="y", tag="y")
+            else:
+                tp = ps_t.tile([P, GROUPS, RT, P], BF16, name="tp", tag="tp")
             for a in range(RT):
                 hc, off = h_of[RT * r + a]
                 for j in range(GROUPS):
@@ -141,31 +159,33 @@ def tile_switchnet_fstar_pb_t_kernel(tc, h_switch, k2, b2, k3, b3, out):
             nc.scalar.copy(out=ht[:], in_=tps[r][:])
             hts[r] = ht
 
-        def stage1(r):
-            for a in range(RT):
+        def mode(r, a):
+            return MODES[(RT * r + a)]
+
+        def stage1(r, aa=(0, 1)):
+            for a in aa:
                 g = ps_g.tile([P, K3], F32, name="g", tag="g")
+                with_b2 = mode(r, a) == "P"
                 for j in range(GROUPS):
-                    nc.tensor.matmul(g[:, j * P:(j + 1) * P], lhsT=hts[r][:, j, a, :], rhs=k2_sb[:, j, :],
-                                     start=True, stop=True)
+                    c = slice(j * P, (j + 1) * P)
+                    if with_b2:
+                        nc.tensor.matmul(g[:, c], lhsT=ones[:], rhs=bz[:, c], start=True, stop=False)
+                    nc.tensor.matmul(g[:, c], lhsT=hts[r][:, j, a, :], rhs=k2_sb[:, j, :],
+                                     start=not with_b2, stop=True)
                 gps[(r, a)] = g
 
         def new_gb(r):
             gbs[r] = gb_pool.tile([P, RT, K3], BF16, name="gb", tag="gb")
 
-        def add_b2_on_vector(r, a):
-            nc.vector.tensor_tensor(
-                out=in_words(gbs[r][:, a, :]), in0=by_words(gps[(r, a)][:]), in1=in_words(b2f[:]), op=ADD)
-
-        def empty_g(r):
-            gs = gs_pool.tile([P, RT, K3], F32, name="gs", tag="gs")
-            for a in range(RT):
-                nc.scalar.copy(out=in_words(gs[:, a, :]), in_=by_words(gps[(r, a)][:]))
-            gss[r] = gs
-
-        def add_b2(r):
-            new_gb(r)
-            nc.gpsimd.tensor_tensor(
-                out=gbs[r][:], in0=gss[r][:], in1=b2f[:].unsqueeze(1).to_broadcast([P, RT, K3]), op=ADD)
+        def empty_g(r, aa=(0, 1)):
+            if 0 in aa:
+                new_gb(r)
+            for a in aa:
+                if mode(r, a) == "P":
+                    nc.scalar.copy(out=in_words(gbs[r][:, a, :]), in_=by_words(gps[(r, a)][:]))
+                if mode(r, a) == "V":
+                    nc.vector.tensor_tensor(
+                        out=in_words(gbs[r][:, a, :]), in0=by_words(gps[(r, a)][:]), in1=in_words(b2f[:]), op=ADD)
 
         def words(r):
             wp = ps_w.tile([P, RT, 2, P], F32, name="wp", tag="wp")
@@ -210,87 +230,102 @@ def tile_switchnet_fstar_pb_t_kernel(tc, h_switch, k2, b2, k3, b3, out):
             a, i = k // 2, k % 2
             if k == 0:
                 ysbs[r] = y_pool.tile([P, RT, L], F32, name="ysb", tag="ysb")
-            nc.vector.tensor_tensor(
-                out=ysbs[r][:, a, i * HALF:(i + 1) * HALF], in0=yps[(r, k)][:],
-                in1=b3f[:, i * HALF:(i + 1) * HALF], op=ADD)
+            ysl = ysbs[r][:, a, i * HALF:(i + 1) * HALF]
+            if YM(r)[k] == "V":
+                nc.vector.tensor_tensor(
+                    out=ysl, in0=yps[(r, k)][:], in1=b3f[:, i * HALF:(i + 1) * HALF], op=ADD)
+            else:
+                nc.scalar.copy(out=ysl, in_=yps[(r, k)][:])
+                for u in range(PIECES):
+                    n = HALF // PIECES
+                    c = slice(i * HALF + u * n, i * HALF + (u + 1) * n)
+                    nc.gpsimd.tensor_tensor(
+                        out=ysbs[r][:, a, c], in0=ysbs[r][:, a, c], in1=b3f[:, c], op=ADD)
             t = RT * r + a
-            if r == ROUNDS - 1 and k == 1:
-                nc.sync.dma_start(out=out_view[:, t:t + 1, :], in_=ysbs[r][:, a:a + 1, :])
             if r == ROUNDS - 1 and k >= 2:
                 nc.sync.dma_start(
                     out=out_view[:, t:t + 1, i * HALF:(i + 1) * HALF],
                     in_=ysbs[r][:, a:a + 1, i * HALF:(i + 1) * HALF])
-            if r < ROUNDS - 1 and k == 3:
+            elif r >= ROUNDS - FINE:
+                if i == 1:
+                    nc.sync.dma_start(out=out_view[:, t:t + 1, :], in_=ysbs[r][:, a:a + 1, :])
+            elif k == 3:
                 nc.sync.dma_start(out=out_view[:, RT * r:RT * (r + 1), :], in_=ysbs[r][:])
 
         yb2 = spread(0)
         yb30 = spread(K3)
-        nc.vector.tensor_copy(out=in_words(b2f[:]), in_=by_words(yb2[:]))
+        nc.scalar.copy(out=in_words(b2f[:]), in_=by_words(yb2[:]))
         nc.scalar.copy(out=b3f[:, 0:HALF], in_=yb30[:])
         transposes(0)
         empty_t(0)
         yb31 = spread(K3 + HALF)
-        stage1(0)
-        nc.scalar.copy(out=b3f[:, HALF:L], in_=yb31[:])
-        transposes(1)
+        transposes(1, True)
         empty_t(1)
+        stage1(0)
+        transposes(2)
+        empty_t(2)
+        nc.scalar.copy(out=b3f[:, HALF:L], in_=yb31[:])
         regroup_k3(0)
         quantise_k3(0)
-        new_gb(0)
-        add_b2_on_vector(0, 0)
-        add_b2_on_vector(0, 1)
+        regroup_k3_on_gpsimd(1, 0, HALF // 2)
+        regroup_k3_on_gpsimd(1, HALF // 2, HALF)
+        empty_g(0)
         words(0)
         empty_w(0)
         stage1(1)
+        transposes(3, True)
+        empty_t(3)
         empty_g(1)
-        add_b2(1)
-        regroup_k3(1)
         quantise(0)
         quantise_k3(1)
-        transposes(2)
-        empty_t(2)
+        words(1)
+        empty_w(1)
         for k in order(0):
             mx_pass(0, k)
         stage1(2)
-        words(1)
-        empty_w(1)
-        empty_g(2)
-        add_b2(2)
-        transposes(3)
-        empty_t(3)
-        stage1(3)
-        empty_g(3)
-        transposes(4)
-        empty_t(4)
         for s in range(ROUNDS):
-            late = s <= 1
             k0, k1, k2_, k3_ = order(s)
-            if s + 2 < ROUNDS and not late:
+            nxt = s + 1 < ROUNDS
+            if s == 0:
+                transposes(4)
+                empty_y(0, k0)
+                empty_y(0, k1)
+                quantise(1)
+                empty_y(0, k2_)
+                empty_y(0, k3_)
+                for k in order(1):
+                    mx_pass(1, k)
+                empty_t(4)
+                empty_g(2)
+                words(2)
+                empty_w(2)
+                stage1(3)
+                continue
+            if s + 3 < ROUNDS and s > 1:
+                stage1(s + 3, (0,))
+            if s + 4 < ROUNDS:
+                transposes(s + 4)
+            if s == 1:
+                empty_g(3)
+                stage1(4, (0,))
+            if s + 2 < ROUNDS and s>0:
                 words(s + 2)
-            if s + 5 < ROUNDS:
-                transposes(s + 5)
-            if s + 2 < ROUNDS and not late:
-                empty_w(s + 2)
-            if s + 5 < ROUNDS:
-                empty_t(s + 5)
+            if s + 3 < ROUNDS:
+                stage1(s + 3, (1,))
+            if nxt:
+                quantise(s + 1)
             empty_y(s, k0)
             empty_y(s, k1)
-            if s + 1 < ROUNDS:
-                quantise(s + 1)
-            if s + 3 < ROUNDS:
-                add_b2(s + 3)
-            if s + 4 < ROUNDS:
-                stage1(s + 4)
-                empty_g(s + 4)
-            if s + 1 < ROUNDS:
-                mx_pass(s + 1, 0)
-                mx_pass(s + 1, 1)
             empty_y(s, k2_)
-            if s + 1 < ROUNDS:
-                mx_pass(s + 1, 2)
             empty_y(s, k3_)
-            if s + 1 < ROUNDS:
-                mx_pass(s + 1, 3)
-            if s + 2 < ROUNDS and late:
-                words(s + 2)
+            if s + 4 < ROUNDS:
+                empty_t(s + 4)
+            if s + 2 < ROUNDS:
                 empty_w(s + 2)
+            if s + 3 < ROUNDS and s > 1:
+                empty_g(s + 3)
+            if s == 1:
+                empty_g(4)
+            if nxt:
+                for k in order(s + 1):
+                    mx_pass(s + 1, k)

@@ -24,12 +24,13 @@ L = 1024
 HALF = 512
 H_CHUNKS = [2, 2, 4, 8, 8, 8]
 PIECES = 1
-FINE = 3
-MODES = "VV" * 16
+WAKE = 2
+FINE = 16
+MODES = "VVVV" + "VPVV" * 7
 
 
 def YM(r):
-    return "VVVV" if r < 1 else ("VSVS" if r < 15 else "SVVV")
+    return "VSVV"
 
 
 FLOPS = 2 * SAMPLES * GROUPS * P * P + 2 * SAMPLES * GROUPS * P * L
@@ -96,7 +97,7 @@ def tile_switchnet_fstar_pb_t_kernel(tc, h_switch, k2, b2, k3, b3, out):
         for c in range(2, len(H_CHUNKS)):
             load_h(c)
 
-        nc.vector.memset(ones[:], 1.0)
+        nc.gpsimd.memset(ones[:], 1.0)
         nc.vector.memset(warm[:], 0.0)
         masks.make_identity(nc, ident[:])
         masks.make_identity(nc, ident_f[:])
@@ -106,6 +107,11 @@ def tile_switchnet_fstar_pb_t_kernel(tc, h_switch, k2, b2, k3, b3, out):
             yb = ps_y.tile([P, HALF], F32, name="y", tag="y")
             nc.tensor.matmul(yb[:], lhsT=ones[:], rhs=bz[:, c0:c0 + HALF], start=True, stop=True)
             return yb
+
+        def wake():
+            yb = ps_y.tile([P, HALF], F32, name="y", tag="y")
+            for d in range(WAKE):
+                nc.tensor.matmul(yb[:], lhsT=ones[:], rhs=ones[:].unsqueeze(1).to_broadcast([P, 4, P]), start=True, stop=True)
 
         def by_words(ap):
             return ap.rearrange("s (p u e) -> s u p e", u=2, e=2)
@@ -121,8 +127,7 @@ def tile_switchnet_fstar_pb_t_kernel(tc, h_switch, k2, b2, k3, b3, out):
 
         def regroup_k3_on_gpsimd(i, n0, n1):
             nc.gpsimd.tensor_scalar(
-                out=k3g[i][:, n0:n1, :].rearrange("p (c i) t -> p c t i", i=4),
-                in0=k3r[i][:, :, n0:n1].rearrange("p t (c i) -> p c t i", i=4),
+                out=k3g[i][:, n0:n1, :], in0=k3r[i][:, :, n0:n1].rearrange("p t n -> p n t"),
                 scalar1=1.0, scalar2=0.0, op0=MULT, op1=ADD)
 
         def quantise_k3(i):
@@ -252,63 +257,47 @@ def tile_switchnet_fstar_pb_t_kernel(tc, h_switch, k2, b2, k3, b3, out):
             elif k == 3:
                 nc.sync.dma_start(out=out_view[:, RT * r:RT * (r + 1), :], in_=ysbs[r][:])
 
+        wake()
         yb2 = spread(0)
-        yb30 = spread(K3)
         nc.scalar.copy(out=in_words(b2f[:]), in_=by_words(yb2[:]))
-        nc.scalar.copy(out=b3f[:, 0:HALF], in_=yb30[:])
         transposes(0)
         empty_t(0)
-        yb31 = spread(K3 + HALF)
+        yb30 = spread(K3)
         transposes(1, True)
-        empty_t(1)
         stage1(0)
+        empty_t(1)
+        nc.scalar.copy(out=b3f[:, 0:HALF], in_=yb30[:])
+        yb31 = spread(K3 + HALF)
         transposes(2)
         empty_t(2)
         nc.scalar.copy(out=b3f[:, HALF:L], in_=yb31[:])
         regroup_k3(0)
+        empty_g(0)
         quantise_k3(0)
         regroup_k3_on_gpsimd(1, 0, HALF // 2)
         regroup_k3_on_gpsimd(1, HALF // 2, HALF)
-        empty_g(0)
+        stage1(1)
         words(0)
         empty_w(0)
-        stage1(1)
+        empty_g(1)
         transposes(3, True)
         empty_t(3)
-        empty_g(1)
         quantise(0)
         quantise_k3(1)
+        stage1(2)
         words(1)
         empty_w(1)
         for k in order(0):
             mx_pass(0, k)
-        stage1(2)
+        empty_g(2)
         for s in range(ROUNDS):
             k0, k1, k2_, k3_ = order(s)
             nxt = s + 1 < ROUNDS
-            if s == 0:
-                transposes(4)
-                empty_y(0, k0)
-                empty_y(0, k1)
-                quantise(1)
-                empty_y(0, k2_)
-                empty_y(0, k3_)
-                for k in order(1):
-                    mx_pass(1, k)
-                empty_t(4)
-                empty_g(2)
-                words(2)
-                empty_w(2)
-                stage1(3)
-                continue
-            if s + 3 < ROUNDS and s > 1:
+            if s + 3 < ROUNDS:
                 stage1(s + 3, (0,))
             if s + 4 < ROUNDS:
                 transposes(s + 4)
-            if s == 1:
-                empty_g(3)
-                stage1(4, (0,))
-            if s + 2 < ROUNDS and s>0:
+            if s + 2 < ROUNDS:
                 words(s + 2)
             if s + 3 < ROUNDS:
                 stage1(s + 3, (1,))
@@ -322,10 +311,8 @@ def tile_switchnet_fstar_pb_t_kernel(tc, h_switch, k2, b2, k3, b3, out):
                 empty_t(s + 4)
             if s + 2 < ROUNDS:
                 empty_w(s + 2)
-            if s + 3 < ROUNDS and s > 1:
+            if s + 3 < ROUNDS:
                 empty_g(s + 3)
-            if s == 1:
-                empty_g(4)
             if nxt:
                 for k in order(s + 1):
                     mx_pass(s + 1, k)

@@ -26,11 +26,11 @@ H_CHUNKS = [2, 2, 4, 8, 8, 8]
 PIECES = 1
 WAKE = 2
 FINE = 16
-MODES = "VVVV" + "VPVV" * 7
+MODES = "VVVP" * 8
 
 
 def YM(r):
-    return "VSVV"
+    return "VSVV" if r < 14 else "VVVV"
 
 
 FLOPS = 2 * SAMPLES * GROUPS * P * P + 2 * SAMPLES * GROUPS * P * L
@@ -119,10 +119,10 @@ def tile_switchnet_fstar_pb_t_kernel(tc, h_switch, k2, b2, k3, b3, out):
         def in_words(ap):
             return ap.rearrange("s (u p e) -> s u p e", u=2, e=2)
 
-        def regroup_k3(i):
+        def regroup_k3(i, n0=0, n1=HALF):
             nc.vector.tensor_copy(
-                out=k3g[i][:].rearrange("p (c i) t -> p c t i", i=4),
-                in_=k3r[i][:].rearrange("p t (c i) -> p c t i", i=4),
+                out=k3g[i][:, n0:n1, :].rearrange("p (c i) t -> p c t i", i=4),
+                in_=k3r[i][:, :, n0:n1].rearrange("p t (c i) -> p c t i", i=4),
             )
 
         def regroup_k3_on_gpsimd(i, n0, n1):
@@ -263,30 +263,32 @@ def tile_switchnet_fstar_pb_t_kernel(tc, h_switch, k2, b2, k3, b3, out):
         transposes(0)
         empty_t(0)
         yb30 = spread(K3)
+        nc.scalar.copy(out=b3f[:, 0:HALF], in_=yb30[:])
         transposes(1, True)
         stage1(0)
         empty_t(1)
-        nc.scalar.copy(out=b3f[:, 0:HALF], in_=yb30[:])
         yb31 = spread(K3 + HALF)
-        transposes(2)
-        empty_t(2)
         nc.scalar.copy(out=b3f[:, HALF:L], in_=yb31[:])
         regroup_k3(0)
+        regroup_k3(1, 0, HALF // 2)
         empty_g(0)
-        quantise_k3(0)
-        regroup_k3_on_gpsimd(1, 0, HALF // 2)
-        regroup_k3_on_gpsimd(1, HALF // 2, HALF)
-        stage1(1)
+        stage1(1, (0,))
         words(0)
+        empty_g(1, (0,))
         empty_w(0)
-        empty_g(1)
-        transposes(3, True)
-        empty_t(3)
+        stage1(1, (1,))
+        empty_g(1, (1,))
+        regroup_k3(1, HALF // 2, HALF)
+        quantise_k3(0)
         quantise(0)
         quantise_k3(1)
-        stage1(2)
+        transposes(2)
+        empty_t(2)
         words(1)
         empty_w(1)
+        transposes(3, True)
+        empty_t(3)
+        stage1(2)
         for k in order(0):
             mx_pass(0, k)
         empty_g(2)

@@ -23,7 +23,7 @@ ROUNDS = TILES // RT
 L = 1024
 HALF = 512
 H_CHUNKS = [2, 2, 4, 8, 8, 8]
-PIECES = 1
+SPLIT = 384
 WAKE = 2
 FINE = 16
 MODES = "VVVP" * 8
@@ -60,6 +60,7 @@ def tile_switchnet_fstar_pb_t_kernel(tc, h_switch, k2, b2, k3, b3, out):
         ones = const.tile([P, P], BF16, name="ones")
         ident = const.tile([P, P], BF16, name="ident")
         ident_f = const.tile([P, P], F32, name="identf")
+        tick = const.tile([P, 1], U32, name="tick")
         warm = const.tile([P, 2], F32, name="warm")
 
         h_of = []
@@ -87,11 +88,11 @@ def tile_switchnet_fstar_pb_t_kernel(tc, h_switch, k2, b2, k3, b3, out):
             nc.sync.dma_start(out=k3r[i][:], in_=k3_view[:, :, i * HALF:(i + 1) * HALF])
 
         nc.vector.memset(bz[:].bitcast(I32), 0)
+        load_h(0)
+        load_k3(0)
         nc.sync.dma_start(out=bz[0:1, 0:K3], in_=b2.rearrange("o j r -> o (j r)"))
         nc.sync.dma_start(out=bz[0:1, K3:K3 + L], in_=b3.rearrange("o j l -> (o j) l"))
-        load_h(0)
         nc.sync.dma_start(out=k2_sb[:], in_=k2.rearrange("j k m -> k j m"))
-        load_k3(0)
         load_h(1)
         load_k3(1)
         for c in range(2, len(H_CHUNKS)):
@@ -150,18 +151,22 @@ def tile_switchnet_fstar_pb_t_kernel(tc, h_switch, k2, b2, k3, b3, out):
 
         def transposes(r, spare=False):
             if spare:
-                tp = ps_y.tile([P, GROUPS, RT, P], BF16, name="y", tag="y")
+                tp = ps_y.tile([P, RT, GROUPS, P], BF16, name="y", tag="y")
             else:
-                tp = ps_t.tile([P, GROUPS, RT, P], BF16, name="tp", tag="tp")
+                tp = ps_t.tile([P, RT, GROUPS, P], BF16, name="tp", tag="tp")
             for a in range(RT):
                 hc, off = h_of[RT * r + a]
                 for j in range(GROUPS):
-                    nc.tensor.transpose(tp[:, j, a, :], hc[:, off, j * P:(j + 1) * P], ident[:])
+                    nc.tensor.transpose(tp[:, a, j, :], hc[:, off, j * P:(j + 1) * P], ident[:])
             tps[r] = tp
 
-        def empty_t(r):
-            ht = ht_pool.tile([P, GROUPS, RT, P], BF16, name="ht", tag="ht")
-            nc.scalar.copy(out=ht[:], in_=tps[r][:])
+        def empty_t(r, by_tile=False):
+            ht = ht_pool.tile([P, RT, GROUPS, P], BF16, name="ht", tag="ht")
+            if by_tile:
+                for a in range(RT):
+                    nc.scalar.copy(out=ht[:, a, :, :], in_=tps[r][:, a, :, :])
+            else:
+                nc.scalar.copy(out=ht[:], in_=tps[r][:])
             hts[r] = ht
 
         def mode(r, a):
@@ -175,7 +180,7 @@ def tile_switchnet_fstar_pb_t_kernel(tc, h_switch, k2, b2, k3, b3, out):
                     c = slice(j * P, (j + 1) * P)
                     if with_b2:
                         nc.tensor.matmul(g[:, c], lhsT=ones[:], rhs=bz[:, c], start=True, stop=False)
-                    nc.tensor.matmul(g[:, c], lhsT=hts[r][:, j, a, :], rhs=k2_sb[:, j, :],
+                    nc.tensor.matmul(g[:, c], lhsT=hts[r][:, a, j, :], rhs=k2_sb[:, j, :],
                                      start=not with_b2, stop=True)
                 gps[(r, a)] = g
 
@@ -213,6 +218,9 @@ def tile_switchnet_fstar_pb_t_kernel(tc, h_switch, k2, b2, k3, b3, out):
             nc.vector.quantize_mx(out=codes[:].bitcast(FP8X4), scales=scl[:], in_=grps[r][:])
             qs[r] = (codes, scl)
 
+        def after_quantise(r):
+            nc.gpsimd.tensor_copy(out=tick[:], in_=qs[r][0][:, 0:1])
+
         def mx_pass(r, k):
             a, i = k // 2, k % 2
             codes, scl = qs[r]
@@ -236,16 +244,15 @@ def tile_switchnet_fstar_pb_t_kernel(tc, h_switch, k2, b2, k3, b3, out):
             if k == 0:
                 ysbs[r] = y_pool.tile([P, RT, L], F32, name="ysb", tag="ysb")
             ysl = ysbs[r][:, a, i * HALF:(i + 1) * HALF]
-            if YM(r)[k] == "V":
+            cut = {"V": HALF, "S": 0, "H": SPLIT}[YM(r)[k]]
+            if cut > 0:
                 nc.vector.tensor_tensor(
-                    out=ysl, in0=yps[(r, k)][:], in1=b3f[:, i * HALF:(i + 1) * HALF], op=ADD)
-            else:
-                nc.scalar.copy(out=ysl, in_=yps[(r, k)][:])
-                for u in range(PIECES):
-                    n = HALF // PIECES
-                    c = slice(i * HALF + u * n, i * HALF + (u + 1) * n)
-                    nc.gpsimd.tensor_tensor(
-                        out=ysbs[r][:, a, c], in0=ysbs[r][:, a, c], in1=b3f[:, c], op=ADD)
+                    out=ysl[:, 0:cut], in0=yps[(r, k)][:, 0:cut], in1=b3f[:, i * HALF:i * HALF + cut], op=ADD)
+            if cut < HALF:
+                c = slice(i * HALF + cut, (i + 1) * HALF)
+                nc.scalar.copy(out=ysl[:, cut:HALF], in_=yps[(r, k)][:, cut:HALF])
+                nc.gpsimd.tensor_tensor(
+                    out=ysbs[r][:, a, c], in0=ysbs[r][:, a, c], in1=b3f[:, c], op=ADD)
             t = RT * r + a
             if r == ROUNDS - 1 and k >= 2:
                 nc.sync.dma_start(
@@ -258,19 +265,18 @@ def tile_switchnet_fstar_pb_t_kernel(tc, h_switch, k2, b2, k3, b3, out):
                 nc.sync.dma_start(out=out_view[:, RT * r:RT * (r + 1), :], in_=ysbs[r][:])
 
         wake()
+        transposes(0)
+        empty_t(0, True)
         yb2 = spread(0)
         nc.scalar.copy(out=in_words(b2f[:]), in_=by_words(yb2[:]))
-        transposes(0)
-        empty_t(0)
+        stage1(0)
+        transposes(1, True)
+        empty_t(1)
         yb30 = spread(K3)
         nc.scalar.copy(out=b3f[:, 0:HALF], in_=yb30[:])
-        transposes(1, True)
-        stage1(0)
-        empty_t(1)
         yb31 = spread(K3 + HALF)
         nc.scalar.copy(out=b3f[:, HALF:L], in_=yb31[:])
         regroup_k3(0)
-        regroup_k3(1, 0, HALF // 2)
         empty_g(0)
         stage1(1, (0,))
         words(0)
@@ -278,7 +284,8 @@ def tile_switchnet_fstar_pb_t_kernel(tc, h_switch, k2, b2, k3, b3, out):
         empty_w(0)
         stage1(1, (1,))
         empty_g(1, (1,))
-        regroup_k3(1, HALF // 2, HALF)
+        regroup_k3_on_gpsimd(1, 0, HALF // 2)
+        regroup_k3_on_gpsimd(1, HALF // 2, HALF)
         quantise_k3(0)
         quantise(0)
         quantise_k3(1)
@@ -303,12 +310,11 @@ def tile_switchnet_fstar_pb_t_kernel(tc, h_switch, k2, b2, k3, b3, out):
                 words(s + 2)
             if s + 3 < ROUNDS:
                 stage1(s + 3, (1,))
-            if nxt:
-                quantise(s + 1)
-            empty_y(s, k0)
-            empty_y(s, k1)
-            empty_y(s, k2_)
-            empty_y(s, k3_)
+            for n, k in enumerate(order(s)):
+                if n == 0 and nxt:
+                    quantise(s + 1)
+                    after_quantise(s + 1)
+                empty_y(s, k)
             if s + 4 < ROUNDS:
                 empty_t(s + 4)
             if s + 2 < ROUNDS:

@@ -23,14 +23,14 @@ ROUNDS = TILES // RT
 L = 1024
 HALF = 512
 H_CHUNKS = [2, 2, 4, 8, 8, 8]
-SPLIT = 384
+SPLIT = 128
 WAKE = 2
 FINE = 16
-MODES = "VVVP" * 8
+MODES = "VVVV" + "VVVP" * 7
 
 
 def YM(r):
-    return "VSVV" if r < 14 else "VVVV"
+    return "VVSH" if r < 14 else "VVVV"
 
 
 FLOPS = 2 * SAMPLES * GROUPS * P * P + 2 * SAMPLES * GROUPS * P * L
@@ -243,16 +243,19 @@ def tile_switchnet_fstar_pb_t_kernel(tc, h_switch, k2, b2, k3, b3, out):
             a, i = k // 2, k % 2
             if k == 0:
                 ysbs[r] = y_pool.tile([P, RT, L], F32, name="ysb", tag="ysb")
-            ysl = ysbs[r][:, a, i * HALF:(i + 1) * HALF]
-            cut = {"V": HALF, "S": 0, "H": SPLIT}[YM(r)[k]]
+            y = yps[(r, k)]
+            lo = i * HALF
+            cut = {"V": 0, "S": HALF, "H": SPLIT}[YM(r)[k]]
             if cut > 0:
-                nc.vector.tensor_tensor(
-                    out=ysl[:, 0:cut], in0=yps[(r, k)][:, 0:cut], in1=b3f[:, i * HALF:i * HALF + cut], op=ADD)
+                nc.scalar.copy(out=ysbs[r][:, a, lo:lo + cut], in_=y[:, 0:cut])
             if cut < HALF:
-                c = slice(i * HALF + cut, (i + 1) * HALF)
-                nc.scalar.copy(out=ysl[:, cut:HALF], in_=yps[(r, k)][:, cut:HALF])
+                nc.vector.tensor_tensor(
+                    out=ysbs[r][:, a, lo + cut:lo + HALF], in0=y[:, cut:HALF], in1=b3f[:, lo + cut:lo + HALF], op=ADD)
+            if cut > 0 and (k == 3 or YM(r)[k + 1] == "V"):
+                lo = 0 if YM(r)[k] == "H" else lo
+                hi = i * HALF + cut
                 nc.gpsimd.tensor_tensor(
-                    out=ysbs[r][:, a, c], in0=ysbs[r][:, a, c], in1=b3f[:, c], op=ADD)
+                    out=ysbs[r][:, a, lo:hi], in0=ysbs[r][:, a, lo:hi], in1=b3f[:, lo:hi], op=ADD)
             t = RT * r + a
             if r == ROUNDS - 1 and k >= 2:
                 nc.sync.dma_start(

@@ -24,7 +24,7 @@ L = 1024
 HALF = 512
 H_CHUNKS = [2, 2, 4, 8, 8, 8]
 SPLIT = 128
-WAKE = 2
+WAKE = 4
 FINE = 16
 MODES = "VVVV" + "VVVP" * 7
 
@@ -74,9 +74,9 @@ def tile_switchnet_fstar_pb_t_kernel(tc, h_switch, k2, b2, k3, b3, out):
             t0 += n
         k2_sb = const.tile([P, GROUPS, P], BF16, name="k2sb")
         k3r = [const.tile([P, GROUPS, HALF], BF16, name="k3r%d" % i) for i in range(2)]
-        k3g = [const.tile([P, HALF, GROUPS], BF16, name="k3g%d" % i, align_bytes=64) for i in range(2)]
-        k3c = const.tile([P, L], U32, name="k3c", align_bytes=64)
-        k3s = const.tile([P, L], U8, name="k3s", align_bytes=64)
+        k3g = [const.tile([P, HALF, GROUPS], BF16, name="k3g%d" % i, align_bytes=256) for i in range(2)]
+        k3c = const.tile([P, L], U32, name="k3c", align_bytes=256)
+        k3s = const.tile([P, L], U8, name="k3s", align_bytes=256)
         b2f = const.tile([P, K3], F32, name="b2f")
         b3f = const.tile([P, L], F32, name="b3f")
 
@@ -176,12 +176,11 @@ def tile_switchnet_fstar_pb_t_kernel(tc, h_switch, k2, b2, k3, b3, out):
             for a in aa:
                 g = ps_g.tile([P, K3], F32, name="g", tag="g")
                 with_b2 = mode(r, a) == "P"
+                if with_b2:
+                    nc.tensor.matmul(g[:], lhsT=ones[:], rhs=bz[:, 0:K3], start=True, stop=False)
                 for j in range(GROUPS):
-                    c = slice(j * P, (j + 1) * P)
-                    if with_b2:
-                        nc.tensor.matmul(g[:, c], lhsT=ones[:], rhs=bz[:, c], start=True, stop=False)
-                    nc.tensor.matmul(g[:, c], lhsT=hts[r][:, a, j, :], rhs=k2_sb[:, j, :],
-                                     start=not with_b2, stop=True)
+                    nc.tensor.matmul(g[:, j * P:(j + 1) * P], lhsT=hts[r][:, a, j, :], rhs=k2_sb[:, j, :],
+                                     start=not with_b2, stop=not with_b2 or j == GROUPS - 1)
                 gps[(r, a)] = g
 
         def new_gb(r):
@@ -206,15 +205,15 @@ def tile_switchnet_fstar_pb_t_kernel(tc, h_switch, k2, b2, k3, b3, out):
             wps[r] = wp
 
         def empty_w(r):
-            grp = grp_pool.tile([P, RT * P * 4], BF16, name="grp", tag="grp", align_bytes=64)
+            grp = grp_pool.tile([P, RT * P * 4], BF16, name="grp", tag="grp", align_bytes=256)
             nc.scalar.copy(
                 out=grp[:].bitcast(F32).rearrange("p (a s u) -> p a s u", a=RT, u=2),
                 in_=wps[r][:].rearrange("p a u s -> p a s u"))
             grps[r] = grp
 
         def quantise(r):
-            codes = q_pool.tile([P, RB], U32, name="codes", tag="codes", align_bytes=64)
-            scl = q_pool.tile([P, RB], U8, name="scl", tag="scl", align_bytes=64)
+            codes = q_pool.tile([P, RB], U32, name="codes", tag="codes", align_bytes=256)
+            scl = q_pool.tile([P, RB], U8, name="scl", tag="scl", align_bytes=256)
             nc.vector.quantize_mx(out=codes[:].bitcast(FP8X4), scales=scl[:], in_=grps[r][:])
             qs[r] = (codes, scl)
 

@@ -126,6 +126,11 @@ def tile_switchnet_fstar_pb_t_kernel(tc, h_switch, k2, b2, k3, b3, out):
                 in_=k3r[i][:, :, n0:n1].rearrange("p t (c i) -> p c t i", i=4),
             )
 
+        def regroup_k3_on_scalar(i, n0, n1):
+            nc.scalar.copy(
+                out=k3g[i][:, n0:n1, :].rearrange("p (c i) t -> p c t i", i=4),
+                in_=k3r[i][:, :, n0:n1].rearrange("p t (c i) -> p c t i", i=4))
+
         def regroup_k3_on_gpsimd(i, n0, n1):
             nc.gpsimd.tensor_scalar(
                 out=k3g[i][:, n0:n1, :], in0=k3r[i][:, :, n0:n1].rearrange("p t n -> p n t"),
@@ -275,24 +280,24 @@ def tile_switchnet_fstar_pb_t_kernel(tc, h_switch, k2, b2, k3, b3, out):
         transposes(1, True)
         empty_t(1)
         yb30 = spread(K3)
-        nc.scalar.copy(out=b3f[:, 0:HALF], in_=yb30[:])
         yb31 = spread(K3 + HALF)
-        nc.scalar.copy(out=b3f[:, HALF:L], in_=yb31[:])
         regroup_k3(0)
+        regroup_k3_on_gpsimd(1, 0, HALF // 2)
+        regroup_k3_on_scalar(1, HALF // 2, HALF)
         empty_g(0)
+        nc.vector.tensor_copy(out=b3f[:, 0:HALF], in_=yb30[:])
         stage1(1, (0,))
         words(0)
         empty_g(1, (0,))
         empty_w(0)
         stage1(1, (1,))
         empty_g(1, (1,))
-        regroup_k3_on_gpsimd(1, 0, HALF // 2)
-        regroup_k3_on_gpsimd(1, HALF // 2, HALF)
         quantise_k3(0)
         quantise(0)
         quantise_k3(1)
         transposes(2)
         empty_t(2)
+        nc.scalar.copy(out=b3f[:, HALF:L], in_=yb31[:])
         words(1)
         empty_w(1)
         transposes(3, True)
@@ -315,7 +320,6 @@ def tile_switchnet_fstar_pb_t_kernel(tc, h_switch, k2, b2, k3, b3, out):
             for n, k in enumerate(order(s)):
                 if n == 0 and nxt:
                     quantise(s + 1)
-                    after_quantise(s + 1)
                 empty_y(s, k)
             if s + 4 < ROUNDS:
                 empty_t(s + 4)

@@ -23,7 +23,7 @@ ROUNDS = TILES // RT
 L = 1024
 HALF = 512
 H_CHUNKS = [2, 2, 4, 8, 8, 8]
-SPLIT = 128
+SPLIT = 64
 WAKE = 4
 FINE = 16
 MODES = "VVVV" + "VVVP" * 7
@@ -282,8 +282,8 @@ def tile_switchnet_fstar_pb_t_kernel(tc, h_switch, k2, b2, k3, b3, out):
         yb30 = spread(K3)
         yb31 = spread(K3 + HALF)
         regroup_k3(0)
-        regroup_k3_on_gpsimd(1, 0, HALF // 2)
-        regroup_k3_on_scalar(1, HALF // 2, HALF)
+        regroup_k3_on_gpsimd(1, 0, 3 * P)
+        regroup_k3_on_scalar(1, 3 * P, HALF)
         empty_g(0)
         nc.vector.tensor_copy(out=b3f[:, 0:HALF], in_=yb30[:])
         stage1(1, (0,))

from contextlib import ExitStack

import concourse.masks as masks
import concourse.mybir as mybir

BF16 = mybir.dt.bfloat16
F32 = mybir.dt.float32
U32 = mybir.dt.uint32
U8 = mybir.dt.uint8
I32 = mybir.dt.int32
FP8X4 = mybir.dt.float8_e4m3fn_x4
ADD = mybir.AluOpType.add
MULT = mybir.AluOpType.mult

P = 128
GROUPS = 4
K3 = GROUPS * P
SAMPLES = 4096
TILES = SAMPLES // P
RT = 2
RB = RT * P
ROUNDS = TILES // RT
L = 1024
HALF = 512
H_CHUNKS = [2, 2, 4, 8, 8, 8]
SPLIT = 64
WAKE = 4
FINE = 16
MODES = "VVVV" + "VVVP" * 7


def YM(r):
    return "VVSH" if r < 14 else "VVVV"


FLOPS = 2 * SAMPLES * GROUPS * P * P + 2 * SAMPLES * GROUPS * P * L


def tile_switchnet_fstar_pb_t_kernel(tc, h_switch, k2, b2, k3, b3, out):
    nc = tc.nc
    h_view = h_switch.rearrange("(p t) j r -> p t (j r)", t=TILES)
    out_view = out.rearrange("(p t) x y c -> p t (x y c)", t=TILES)
    k3_view = k3.rearrange("o (p j) n -> p (o j) n", j=4)

    with ExitStack() as ctx:
        ctx.enter_context(tc.manual_schedule())
        const = ctx.enter_context(tc.tile_pool(name="const", bufs=1))
        ht_pool = ctx.enter_context(tc.tile_pool(name="ht", bufs=3))
        gs_pool = ctx.enter_context(tc.tile_pool(name="gs", bufs=3))
        gb_pool = ctx.enter_context(tc.tile_pool(name="gb", bufs=3))
        grp_pool = ctx.enter_context(tc.tile_pool(name="grp", bufs=3))
        q_pool = ctx.enter_context(tc.tile_pool(name="q", bufs=3))
        y_pool = ctx.enter_context(tc.tile_pool(name="ysb", bufs=5))
        ps_t = ctx.enter_context(tc.psum_pool(name="pst", bufs=1))
        ps_g = ctx.enter_context(tc.psum_pool(name="psg", bufs=2))
        ps_w = ctx.enter_context(tc.psum_pool(name="psw", bufs=1))
        ps_y = ctx.enter_context(tc.psum_pool(name="psy", bufs=4))

        bz = const.tile([P, K3 + L], BF16, name="bz")
        ones = const.tile([P, P], BF16, name="ones")
        ident = const.tile([P, P], BF16, name="ident")
        ident_f = const.tile([P, P], F32, name="identf")
        tick = const.tile([P, 1], U32, name="tick")
        warm = const.tile([P, 2], F32, name="warm")

        h_of = []
        h_tiles = []
        t0 = 0
        for c, n in enumerate(H_CHUNKS):
            hc = const.tile([P, n, GROUPS * P], BF16, name="h%d" % c)
            h_tiles.append((hc, t0, n))
            for i in range(n):
                h_of.append((hc, i))
            t0 += n
        k2_sb = const.tile([P, GROUPS, P], BF16, name="k2sb")
        k3r = [const.tile([P, GROUPS, HALF], BF16, name="k3r%d" % i) for i in range(2)]
        k3g = [const.tile([P, HALF, GROUPS], BF16, name="k3g%d" % i, align_bytes=256) for i in range(2)]
        k3c = const.tile([P, L], U32, name="k3c", align_bytes=256)
        k3s = const.tile([P, L], U8, name="k3s", align_bytes=256)
        b2f = const.tile([P, K3], F32, name="b2f")
        b3f = const.tile([P, L], F32, name="b3f")

        def load_h(c):
            hc, start, n = h_tiles[c]
            nc.sync.dma_start(out=hc[:], in_=h_view[:, start:start + n, :])

        def load_k3(i):
            nc.sync.dma_start(out=k3r[i][:], in_=k3_view[:, :, i * HALF:(i + 1) * HALF])

        nc.vector.memset(bz[:].bitcast(I32), 0)
        load_h(0)
        load_k3(0)
        nc.sync.dma_start(out=bz[0:1, 0:K3], in_=b2.rearrange("o j r -> o (j r)"))
        nc.sync.dma_start(out=bz[0:1, K3:K3 + L], in_=b3.rearrange("o j l -> (o j) l"))
        nc.sync.dma_start(out=k2_sb[:], in_=k2.rearrange("j k m -> k j m"))
        load_h(1)
        load_k3(1)
        for c in range(2, len(H_CHUNKS)):
            load_h(c)

        nc.gpsimd.memset(ones[:], 1.0)
        nc.vector.memset(warm[:], 0.0)
        masks.make_identity(nc, ident[:])
        masks.make_identity(nc, ident_f[:])
        nc.scalar.copy(out=warm[:, 1:2], in_=warm[:, 0:1])

        def spread(c0):
            yb = ps_y.tile([P, HALF], F32, name="y", tag="y")
            nc.tensor.matmul(yb[:], lhsT=ones[:], rhs=bz[:, c0:c0 + HALF], start=True, stop=True)
            return yb

        def wake():
            yb = ps_y.tile([P, HALF], F32, name="y", tag="y")
            for d in range(WAKE):
                nc.tensor.matmul(yb[:], lhsT=ones[:], rhs=ones[:].unsqueeze(1).to_broadcast([P, 4, P]), start=True, stop=True)

        def by_words(ap):
            return ap.rearrange("s (p u e) -> s u p e", u=2, e=2)

        def in_words(ap):
            return ap.rearrange("s (u p e) -> s u p e", u=2, e=2)

        def regroup_k3(i, n0=0, n1=HALF):
            nc.vector.tensor_copy(
                out=k3g[i][:, n0:n1, :].rearrange("p (c i) t -> p c t i", i=4),
                in_=k3r[i][:, :, n0:n1].rearrange("p t (c i) -> p c t i", i=4),
            )

        def regroup_k3_on_scalar(i, n0, n1):
            nc.scalar.copy(
                out=k3g[i][:, n0:n1, :].rearrange("p (c i) t -> p c t i", i=4),
                in_=k3r[i][:, :, n0:n1].rearrange("p t (c i) -> p c t i", i=4))

        def regroup_k3_on_gpsimd(i, n0, n1):
            nc.gpsimd.tensor_scalar(
                out=k3g[i][:, n0:n1, :], in0=k3r[i][:, :, n0:n1].rearrange("p t n -> p n t"),
                scalar1=1.0, scalar2=0.0, op0=MULT, op1=ADD)

        def quantise_k3(i):
            nc.vector.quantize_mx(
                out=k3c[:, i * HALF:(i + 1) * HALF].bitcast(FP8X4),
                scales=k3s[:, i * HALF:(i + 1) * HALF],
                in_=k3g[i][:].rearrange("p n t -> p (n t)"),
            )

        tps = {}
        hts = {}
        gps = {}
        gss = {}
        gbs = {}
        wps = {}
        grps = {}
        qs = {}
        yps = {}
        ysbs = {}

        def transposes(r, spare=False):
            if spare:
                tp = ps_y.tile([P, RT, GROUPS, P], BF16, name="y", tag="y")
            else:
                tp = ps_t.tile([P, RT, GROUPS, P], BF16, name="tp", tag="tp")
            for a in range(RT):
                hc, off = h_of[RT * r + a]
                for j in range(GROUPS):
                    nc.tensor.transpose(tp[:, a, j, :], hc[:, off, j * P:(j + 1) * P], ident[:])
            tps[r] = tp

        def empty_t(r, by_tile=False):
            ht = ht_pool.tile([P, RT, GROUPS, P], BF16, name="ht", tag="ht")
            if by_tile:
                for a in range(RT):
                    nc.scalar.copy(out=ht[:, a, :, :], in_=tps[r][:, a, :, :])
            else:
                nc.scalar.copy(out=ht[:], in_=tps[r][:])
            hts[r] = ht

        def mode(r, a):
            return MODES[(RT * r + a)]

        def stage1(r, aa=(0, 1)):
            for a in aa:
                g = ps_g.tile([P, K3], F32, name="g", tag="g")
                with_b2 = mode(r, a) == "P"
                if with_b2:
                    nc.tensor.matmul(g[:], lhsT=ones[:], rhs=bz[:, 0:K3], start=True, stop=False)
                for j in range(GROUPS):
                    nc.tensor.matmul(g[:, j * P:(j + 1) * P], lhsT=hts[r][:, a, j, :], rhs=k2_sb[:, j, :],
                                     start=not with_b2, stop=not with_b2 or j == GROUPS - 1)
                gps[(r, a)] = g

        def new_gb(r):
            gbs[r] = gb_pool.tile([P, RT, K3], BF16, name="gb", tag="gb")

        def empty_g(r, aa=(0, 1)):
            if 0 in aa:
                new_gb(r)
            for a in aa:
                if mode(r, a) == "P":
                    nc.scalar.copy(out=in_words(gbs[r][:, a, :]), in_=by_words(gps[(r, a)][:]))
                if mode(r, a) == "V":
                    nc.vector.tensor_tensor(
                        out=in_words(gbs[r][:, a, :]), in0=by_words(gps[(r, a)][:]), in1=in_words(b2f[:]), op=ADD)

        def words(r):
            wp = ps_w.tile([P, RT, 2, P], F32, name="wp", tag="wp")
            for a in range(RT):
                w = gbs[r][:, a, :].bitcast(F32)
                for u in range(2):
                    nc.tensor.transpose(wp[:, a, u, :], w[:, u * P:(u + 1) * P], ident_f[:])
            wps[r] = wp

        def empty_w(r):
            grp = grp_pool.tile([P, RT * P * 4], BF16, name="grp", tag="grp", align_bytes=256)
            nc.scalar.copy(
                out=grp[:].bitcast(F32).rearrange("p (a s u) -> p a s u", a=RT, u=2),
                in_=wps[r][:].rearrange("p a u s -> p a s u"))
            grps[r] = grp

        def quantise(r):
            codes = q_pool.tile([P, RB], U32, name="codes", tag="codes", align_bytes=256)
            scl = q_pool.tile([P, RB], U8, name="scl", tag="scl", align_bytes=256)
            nc.vector.quantize_mx(out=codes[:].bitcast(FP8X4), scales=scl[:], in_=grps[r][:])
            qs[r] = (codes, scl)

        def after_quantise(r):
            nc.gpsimd.tensor_copy(out=tick[:], in_=qs[r][0][:, 0:1])

        def mx_pass(r, k):
            a, i = k // 2, k % 2
            codes, scl = qs[r]
            y = ps_y.tile([P, HALF], F32, name="y", tag="y")
            nc.tensor.matmul_mx(
                out=y[:],
                lhsT=codes[:, a * P:(a + 1) * P].bitcast(FP8X4),
                lhsT_scale=scl[:, a * P:(a + 1) * P],
                rhs=k3c[:, i * HALF:(i + 1) * HALF].bitcast(FP8X4),
                rhs_scale=k3s[:, i * HALF:(i + 1) * HALF],
                start=True,
                stop=True,
            )
            yps[(r, k)] = y

        def order(r):
            return (0, 2, 1, 3) if r == 0 else (0, 1, 2, 3)

        def empty_y(r, k):
            a, i = k // 2, k % 2
            if k == 0:
                ysbs[r] = y_pool.tile([P, RT, L], F32, name="ysb", tag="ysb")
            y = yps[(r, k)]
            lo = i * HALF
            cut = {"V": 0, "S": HALF, "H": SPLIT}[YM(r)[k]]
            if cut > 0:
                nc.scalar.copy(out=ysbs[r][:, a, lo:lo + cut], in_=y[:, 0:cut])
            if cut < HALF:
                nc.vector.tensor_tensor(
                    out=ysbs[r][:, a, lo + cut:lo + HALF], in0=y[:, cut:HALF], in1=b3f[:, lo + cut:lo + HALF], op=ADD)
            if cut > 0 and (k == 3 or YM(r)[k + 1] == "V"):
                lo = 0 if YM(r)[k] == "H" else lo
                hi = i * HALF + cut
                nc.gpsimd.tensor_tensor(
                    out=ysbs[r][:, a, lo:hi], in0=ysbs[r][:, a, lo:hi], in1=b3f[:, lo:hi], op=ADD)
            t = RT * r + a
            if r == ROUNDS - 1 and k >= 2:
                nc.sync.dma_start(
                    out=out_view[:, t:t + 1, i * HALF:(i + 1) * HALF],
                    in_=ysbs[r][:, a:a + 1, i * HALF:(i + 1) * HALF])
            elif r >= ROUNDS - FINE:
                if i == 1:
                    nc.sync.dma_start(out=out_view[:, t:t + 1, :], in_=ysbs[r][:, a:a + 1, :])
            elif k == 3:
                nc.sync.dma_start(out=out_view[:, RT * r:RT * (r + 1), :], in_=ysbs[r][:])

        wake()
        transposes(0)
        empty_t(0, True)
        yb2 = spread(0)
        nc.scalar.copy(out=in_words(b2f[:]), in_=by_words(yb2[:]))
        stage1(0)
        transposes(1, True)
        empty_t(1)
        yb30 = spread(K3)
        yb31 = spread(K3 + HALF)
        regroup_k3(0)
        regroup_k3_on_gpsimd(1, 0, 3 * P)
        regroup_k3_on_scalar(1, 3 * P, HALF)
        empty_g(0)
        nc.vector.tensor_copy(out=b3f[:, 0:HALF], in_=yb30[:])
        stage1(1, (0,))
        words(0)
        empty_g(1, (0,))
        empty_w(0)
        stage1(1, (1,))
        empty_g(1, (1,))
        quantise_k3(0)
        quantise(0)
        quantise_k3(1)
        transposes(2)
        empty_t(2)
        nc.scalar.copy(out=b3f[:, HALF:L], in_=yb31[:])
        words(1)
        empty_w(1)
        transposes(3, True)
        empty_t(3)
        stage1(2)
        for k in order(0):
            mx_pass(0, k)
        empty_g(2)
        for s in range(ROUNDS):
            k0, k1, k2_, k3_ = order(s)
            nxt = s + 1 < ROUNDS
            if s + 3 < ROUNDS:
                stage1(s + 3, (0,))
            if s + 4 < ROUNDS:
                transposes(s + 4)
            if s + 2 < ROUNDS:
                words(s + 2)
            if s + 3 < ROUNDS:
                stage1(s + 3, (1,))
            for n, k in enumerate(order(s)):
                if n == 0 and nxt:
                    quantise(s + 1)
                empty_y(s, k)
            if s + 4 < ROUNDS:
                empty_t(s + 4)
            if s + 2 < ROUNDS:
                empty_w(s + 2)
            if s + 3 < ROUNDS:
                empty_g(s + 3)
            if nxt:
                for k in order(s + 1):
                    mx_pass(s + 1, k)
